import numpy as np
import ml_dtypes


def mxq(x, axis, fmt="e4m3"):
    dtype, down = {"e4m3": (ml_dtypes.float8_e4m3fn, 7), "e5m2": (ml_dtypes.float8_e5m2, 14)}[fmt]
    v = np.moveaxis(np.asarray(x, np.float32).astype(ml_dtypes.bfloat16).astype(np.float64), axis, -1)
    blocks = v.reshape(v.shape[:-1] + (-1, 32))
    amax = np.abs(blocks).max(-1, keepdims=True)
    byte = np.maximum(np.where(amax > 0, np.frexp(amax)[1] - 1 + 127, 0) - down, 1)
    scale = np.exp2(byte - 127.0)
    codes = (blocks / scale).astype(np.float32).astype(dtype).astype(np.float64)
    return np.moveaxis((codes * scale).reshape(v.shape), -1, axis)


WIDE = False


def mx_kscale(k):
    if not WIDE:
        return np.ones(k)
    levels = np.array([10, -10, 5, -5, 0])
    a = np.random.permutation(np.resize(levels, k // 512 * 4)).reshape(k // 512, 4)
    idx = np.arange(k)
    return np.exp2(a[idx // 512, idx % 128 // 32])


BF16 = ml_dtypes.bfloat16


def bf(x):
    return np.asarray(x, np.float32).astype(BF16)


def f64(x):
    return np.asarray(x).astype(np.float64)


B, R, CIN, N_CAPS, COUT = 256, 1152, 8, 16, 16
K = R * CIN


def squash(t, axis=-1):
    sq = np.sum(t * t, axis=axis, keepdims=True)
    return sq / (1.0 + sq) * t / np.sqrt(sq)


def setup_inputs():
    s = mx_kscale(K).reshape(R, CIN)
    x = np.random.standard_normal((B, R, CIN)) * s
    W = np.random.standard_normal((N_CAPS, R, CIN, COUT)) * np.sqrt(3.0 * R / (CIN * COUT)) / s[:, :, None]
    return {"x": bf(x), "W": bf(W)}


def reference(x, W):
    xq = mxq(f64(x).reshape(B, K), 1, "e4m3")
    wq = mxq(f64(W).reshape(N_CAPS, K, COUT), 1, "e4m3")
    c = 1.0 / R
    s = (c * (xq @ wq))[:, :, None, :]
    v = squash(s, axis=-1)
    return v[:, :, :, None, :]

@@ -1,0 +1,263 @@
+from contextlib import ExitStack
+
+import concourse.masks as masks
+import concourse.mybir as mybir
+
+FLOPS = 2 * 256 * 9216 * 256
+
+F32 = mybir.dt.float32
+BF16 = mybir.dt.bfloat16
+U32 = mybir.dt.uint32
+U8 = mybir.dt.uint8
+FP8X4 = mybir.dt.float8_e4m3fn_x4
+ACT = mybir.ActivationFunctionType
+ALU = mybir.AluOpType
+
+P = 128
+K = 9216
+ROUTES = 1152
+
+
+def pass_of_slot(slot):
+    if slot >= 16:
+        return 9 * (slot - 16) + 8
+    tau, mh = divmod(slot, 8)
+    m, h = divmod(mh, 4)
+    return 9 * m + 4 * tau + h
+
+
+def tile_capsulelayer_kernel(tc, x, W, out):
+    nc = tc.nc
+    with ExitStack() as ctx:
+        const = ctx.enter_context(tc.tile_pool(name="const", bufs=1))
+        raw = ctx.enter_context(tc.tile_pool(name="raw", bufs=1))
+        keep = ctx.enter_context(tc.tile_pool(name="keep", bufs=1))
+        l2p = ctx.enter_context(tc.tile_pool(name="l2p", bufs=6))
+        gwp = ctx.enter_context(tc.tile_pool(name="gwp", bufs=2))
+        gxp = ctx.enter_context(tc.tile_pool(name="gxp", bufs=4))
+        ep = ctx.enter_context(tc.tile_pool(name="ep", bufs=2))
+        tp = ctx.enter_context(tc.psum_pool(name="tp", bufs=6))
+        accp = ctx.enter_context(tc.psum_pool(name="accp", bufs=1))
+
+        ident = const.tile([P, P], F32)
+        masks.make_identity(nc, ident[:])
+        one = const.tile([P, 1], F32)
+        nc.vector.memset(one[:], 1.0)
+        warm = const.tile([P, 1], F32)
+        nc.scalar.activation(out=warm[:], in_=one[:], func=ACT.Sqrt)
+
+        w_raw = [raw.tile([P, 8192], BF16, name="w_raw%d" % t) for t in range(2)]
+        w_rawl = raw.tile([P, 4096], BF16)
+        x_raw = [raw.tile([P, K], BF16, name="x_raw%d" % b) for b in range(2)]
+        wc = keep.tile([P, 18 * 256], U32, align_bytes=64)
+        ws = keep.tile([P, 18 * 256], U8, align_bytes=64)
+        xc = keep.tile([P, 18 * 256], U32, align_bytes=64)
+        xs = keep.tile([P, 18 * 256], U8, align_bytes=64)
+        acc = [accp.tile([P, 256], F32, name="acc%d" % b) for b in range(2)]
+
+        nc.vector.memset(w_rawl[:], 0.0)
+
+        wr = W.rearrange("n (m r) i o -> (n m) (r i o)", m=2)
+        xf = x.rearrange("b r i -> b (r i)")
+
+        def load_w(tau, u, h):
+            c0 = (4 * tau + h) * 8192 + u * 4096
+            nc.sync.dma_start(
+                out=w_raw[tau][h:P:4, u * 4096 : (u + 1) * 4096],
+                in_=wr[:, c0 : c0 + 4096],
+            )
+
+        def load_x(b, g0, g1):
+            nc.sync.dma_start(
+                out=x_raw[b][:, g0 * 512 : g1 * 512],
+                in_=xf[b * P : (b + 1) * P, g0 * 512 : g1 * 512],
+            )
+
+        for u in range(2):
+            for h in range(4):
+                load_w(0, u, h)
+        for u in range(2):
+            c0 = 8 * 8192 + u * 4096
+            nc.sync.dma_start(out=w_rawl[u:P:4, :], in_=wr[:, c0 : c0 + 4096])
+        for m in range(2):
+            for b in range(2):
+                load_x(b, 9 * m, 9 * m + 4)
+        for u in range(2):
+            for h in range(4):
+                load_w(1, u, h)
+        for m in range(2):
+            for b in range(2):
+                load_x(b, 9 * m + 4, 9 * m + 9)
+
+        xw = [x_raw[b][:].bitcast(F32) for b in range(2)]
+
+        def w_main(tau, split_u):
+            gw = gwp.tile([P, 8192], BF16, name="gw%d" % tau, tag="gw", align_bytes=64)
+            gwv = gw[:].bitcast(F32).rearrange("p (m c u) -> p m c u", m=8, c=256, u=2)
+            src = w_raw[tau][:].rearrange("p (u k o) -> p u k o", u=2, k=256, o=16)
+            l2s = []
+            for ob in range(4):
+                l2 = l2p.tile([P, 2048], BF16, name="l2_%d_%d" % (tau, ob), tag="l2")
+                l2s.append(l2)
+            if split_u:
+                for u in range(2):
+                    for ob in range(4):
+                        dst = l2s[ob][:].rearrange("p (u i k) -> p u k i", u=2, i=4, k=256)
+                        nc.vector.tensor_copy(
+                            out=dst[:, u], in_=src[:, u, :, 4 * ob : 4 * ob + 4]
+                        )
+            for ob in range(4):
+                if not split_u:
+                    dst = l2s[ob][:].rearrange("p (u i k) -> p u k i", u=2, i=4, k=256)
+                    nc.vector.tensor_copy(out=dst, in_=src[:, :, :, 4 * ob : 4 * ob + 4])
+                l2w = l2s[ob][:].bitcast(F32)
+                for jj in range(2):
+                    j = 2 * ob + jj
+                    bank = tp.tile([P, 512], F32, name="bw%d_%d" % (tau, j), tag="tp")
+                    for u in range(2):
+                        for oo in range(2):
+                            i = 2 * jj + oo
+                            nc.tensor.transpose(
+                                out=bank[:, (2 * u + oo) * P : (2 * u + oo + 1) * P],
+                                in_=l2w[:, (4 * u + i) * P : (4 * u + i + 1) * P],
+                                identity=ident[:],
+                            )
+                    nc.scalar.copy(
+                        out=gwv[:, :, 32 * j : 32 * j + 32, :],
+                        in_=bank[:].rearrange("p (u c m) -> p m c u", u=2, c=32, m=8),
+                    )
+            for half in range(2):
+                s0 = (8 * tau + 4 * half) * 256
+                nc.vector.quantize_mx(
+                    out=wc[:, s0 : s0 + 1024].bitcast(FP8X4),
+                    scales=ws[:, s0 : s0 + 1024],
+                    in_=gw[:, half * 4096 : (half + 1) * 4096],
+                )
+
+        def w_left():
+            gw = gwp.tile([P, 2048], BF16, name="gwl", tag="gwl", bufs=1, align_bytes=64)
+            gwv = gw[:].bitcast(F32).rearrange("p (m c u) -> p m c u", m=2, c=256, u=2)
+            src = w_rawl[:].rearrange("p (k o) -> p k o", k=256, o=16)
+            for ob in range(4):
+                l2 = l2p.tile([P, 1024], BF16, name="l2_l_%d" % ob, tag="l2")
+                nc.vector.tensor_copy(
+                    out=l2[:].rearrange("p (i k) -> p k i", i=4, k=256),
+                    in_=src[:, :, 4 * ob : 4 * ob + 4],
+                )
+                l2w = l2[:].bitcast(F32)
+                bank = tp.tile([P, 512], F32, name="bwl%d" % ob, tag="tp")
+                for i in range(4):
+                    nc.tensor.transpose(
+                        out=bank[:, i * P : (i + 1) * P],
+                        in_=l2w[:, i * P : (i + 1) * P],
+                        identity=ident[:],
+                    )
+                nc.scalar.copy(
+                    out=gwv[:, :, 64 * ob : 64 * ob + 64, :],
+                    in_=bank[:].rearrange("p (c m q) -> p m c q", c=64, m=2, q=4)[:, :, :, 0:2],
+                )
+            nc.vector.quantize_mx(
+                out=wc[:, 16 * 256 : 18 * 256].bitcast(FP8X4),
+                scales=ws[:, 16 * 256 : 18 * 256],
+                in_=gw[:],
+            )
+
+        def x_off(slot, b):
+            if slot >= 16:
+                return 4096 + b * 256 + (slot - 16) * P
+            gi, sl = divmod(slot, 4)
+            return gi * 1024 + b * 512 + sl * P
+
+        def x_job(slots, b):
+            ns = len(slots)
+            gx = gxp.tile(
+                [P, ns * 512], BF16, name="gx%d_%d" % (slots[0], b), tag="gx", align_bytes=64
+            )
+            gxv = gx[:].bitcast(F32).rearrange("p (s b u) -> p s b u", s=ns, b=P, u=2)
+            for lp in range(ns // 2):
+                bank = tp.tile([P, 512], F32, name="bx%d_%d_%d" % (slots[0], b, lp), tag="tp")
+                for l in range(2):
+                    g = pass_of_slot(slots[2 * lp + l])
+                    for u in range(2):
+                        c0 = 256 * g + P * u
+                        nc.tensor.transpose(
+                            out=bank[:, (2 * l + u) * P : (2 * l + u + 1) * P],
+                            in_=xw[b][:, c0 : c0 + P],
+                            identity=ident[:],
+                        )
+                nc.scalar.copy(
+                    out=gxv[:, 2 * lp : 2 * lp + 2, :, :],
+                    in_=bank[:].rearrange("p (l u b) -> p l b u", l=2, u=2, b=P),
+                )
+            o0 = x_off(slots[0], b)
+            nc.vector.quantize_mx(
+                out=xc[:, o0 : o0 + ns * P].bitcast(FP8X4),
+                scales=xs[:, o0 : o0 + ns * P],
+                in_=gx[:],
+            )
+
+        def mm(slot):
+            for b in range(2):
+                o0 = x_off(slot, b)
+                nc.tensor.matmul_mx(
+                    out=acc[b][:],
+                    lhsT=xc[:, o0 : o0 + P].bitcast(FP8X4),
+                    lhsT_scale=xs[:, o0 : o0 + P],
+                    rhs=wc[:, slot * 256 : (slot + 1) * 256].bitcast(FP8X4),
+                    rhs_scale=ws[:, slot * 256 : (slot + 1) * 256],
+                    start=(slot == 0),
+                    stop=(slot == 17),
+                )
+
+        w_main(0, True)
+        w_left()
+        for m in range(2):
+            for b in range(2):
+                x_job([4 * m + s for s in range(4)], b)
+        for slot in range(8):
+            mm(slot)
+        w_main(1, False)
+        for m in range(2):
+            for b in range(2):
+                x_job([8 + 4 * m + s for s in range(4)], b)
+        for b in range(2):
+            x_job([16, 17], b)
+        for slot in range(8, 18):
+            mm(slot)
+
+        outv = out.rearrange("n b x y o -> b n (x y o)")
+        for b in range(2):
+            s = ep.tile([P, 256], F32, name="s%d" % b, tag="s")
+            sv = s[:].rearrange("p (n o) -> p n o", n=16, o=16)
+            nc.scalar.mul(
+                out=sv,
+                in_=acc[b][:].rearrange("p (o n) -> p n o", o=16, n=16),
+                mul=1.0 / ROUTES,
+            )
+            s2 = ep.tile([P, 256], F32, name="s2_%d" % b, tag="s2")
+            nc.vector.tensor_tensor(out=s2[:], in0=s[:], in1=s[:], op=ALU.mult)
+            sq = ep.tile([P, 16], F32, name="sq%d" % b, tag="sq")
+            nc.vector.tensor_reduce(
+                out=sq[:],
+                in_=s2[:].rearrange("p (n o) -> p n o", n=16, o=16),
+                axis=mybir.AxisListType.X,
+                op=ALU.add,
+            )
+            rt = ep.tile([P, 16], F32, name="rt%d" % b, tag="rt")
+            nc.scalar.activation(out=rt[:], in_=sq[:], func=ACT.Sqrt)
+            den = ep.tile([P, 16], F32, name="den%d" % b, tag="den")
+            nc.vector.tensor_scalar_add(den[:], sq[:], 1.0)
+            nc.vector.reciprocal(den[:], den[:])
+            fac = ep.tile([P, 16], F32, name="fac%d" % b, tag="fac")
+            nc.vector.tensor_tensor(out=fac[:], in0=rt[:], in1=den[:], op=ALU.mult)
+            res = ep.tile([P, 256], F32, name="res%d" % b, tag="res")
+            nc.vector.tensor_tensor(
+                out=res[:].rearrange("p (n o) -> p n o", n=16, o=16),
+                in0=sv,
+                in1=fac[:].unsqueeze(2).to_broadcast([P, 16, 16]),
+                op=ALU.mult,
+            )
+            nc.sync.dma_start(
+                out=outv[b * P : (b + 1) * P],
+                in_=res[:].rearrange("p (n o) -> p n o", n=16, o=16),
+            )

@@ -14,16 +14,10 @@ ACT = mybir.ActivationFunctionType
 ALU = mybir.AluOpType
 
 P = 128
-K = 9216
+HALF_K = 4608
 ROUTES = 1152
-
-
-def pass_of_slot(slot):
-    if slot >= 16:
-        return 9 * (slot - 16) + 8
-    tau, mh = divmod(slot, 8)
-    m, h = divmod(mh, 4)
-    return 9 * m + 4 * tau + h
+STAGES = 5
+LAST = 4
 
 
 def tile_capsulelayer_kernel(tc, x, W, out):
@@ -33,11 +27,12 @@ def tile_capsulelayer_kernel(tc, x, W, out):
         raw = ctx.enter_context(tc.tile_pool(name="raw", bufs=1))
         keep = ctx.enter_context(tc.tile_pool(name="keep", bufs=1))
         l2p = ctx.enter_context(tc.tile_pool(name="l2p", bufs=6))
-        gwp = ctx.enter_context(tc.tile_pool(name="gwp", bufs=2))
-        gxp = ctx.enter_context(tc.tile_pool(name="gxp", bufs=4))
+        gwp = ctx.enter_context(tc.tile_pool(name="gwp", bufs=3))
+        gxp = ctx.enter_context(tc.tile_pool(name="gxp", bufs=6))
         ep = ctx.enter_context(tc.tile_pool(name="ep", bufs=2))
-        tp = ctx.enter_context(tc.psum_pool(name="tp", bufs=6))
+        tp = ctx.enter_context(tc.psum_pool(name="tp", bufs=5))
         accp = ctx.enter_context(tc.psum_pool(name="accp", bufs=1))
+        ctx.enter_context(tc.manual_schedule())
 
         ident = const.tile([P, P], F32)
         masks.make_identity(nc, ident[:])
@@ -46,218 +41,204 @@ def tile_capsulelayer_kernel(tc, x, W, out):
         warm = const.tile([P, 1], F32)
         nc.scalar.activation(out=warm[:], in_=one[:], func=ACT.Sqrt)
 
-        w_raw = [raw.tile([P, 8192], BF16, name="w_raw%d" % t) for t in range(2)]
-        w_rawl = raw.tile([P, 4096], BF16)
-        x_raw = [raw.tile([P, K], BF16, name="x_raw%d" % b) for b in range(2)]
+        w_raw = [raw.tile([P, 4096], BF16, name="w_raw%d" % s) for s in range(STAGES)]
+        x_raw = [
+            [raw.tile([P, HALF_K], BF16, name="x_raw%d_%d" % (b, m)) for m in range(2)]
+            for b in range(2)
+        ]
         wc = keep.tile([P, 18 * 256], U32, align_bytes=64)
         ws = keep.tile([P, 18 * 256], U8, align_bytes=64)
         xc = keep.tile([P, 18 * 256], U32, align_bytes=64)
         xs = keep.tile([P, 18 * 256], U8, align_bytes=64)
         acc = [accp.tile([P, 256], F32, name="acc%d" % b) for b in range(2)]
+        idle = accp.tile([P, P], F32, name="idle")
 
-        nc.vector.memset(w_rawl[:], 0.0)
+        nc.vector.memset(w_raw[LAST][:], 0.0)
 
         wr = W.rearrange("n (m r) i o -> (n m) (r i o)", m=2)
         xf = x.rearrange("b r i -> b (r i)")
 
-        def load_w(tau, u, h):
-            c0 = (4 * tau + h) * 8192 + u * 4096
-            nc.sync.dma_start(
-                out=w_raw[tau][h:P:4, u * 4096 : (u + 1) * 4096],
-                in_=wr[:, c0 : c0 + 4096],
-            )
+        def load_w(s):
+            for q in range(4 if s < LAST else 2):
+                c0 = (4 * s + q) * 4096
+                nc.sync.dma_start(out=w_raw[s][q:P:4, :], in_=wr[:, c0 : c0 + 4096])
 
-        def load_x(b, g0, g1):
-            nc.sync.dma_start(
-                out=x_raw[b][:, g0 * 512 : g1 * 512],
-                in_=xf[b * P : (b + 1) * P, g0 * 512 : g1 * 512],
-            )
-
-        for u in range(2):
-            for h in range(4):
-                load_w(0, u, h)
-        for u in range(2):
-            c0 = 8 * 8192 + u * 4096
-            nc.sync.dma_start(out=w_rawl[u:P:4, :], in_=wr[:, c0 : c0 + 4096])
-        for m in range(2):
+        def load_x(g0, g1):
             for b in range(2):
-                load_x(b, 9 * m, 9 * m + 4)
-        for u in range(2):
-            for h in range(4):
-                load_w(1, u, h)
-        for m in range(2):
-            for b in range(2):
-                load_x(b, 9 * m + 4, 9 * m + 9)
-
-        xw = [x_raw[b][:].bitcast(F32) for b in range(2)]
-
-        def w_main(tau, split_u):
-            gw = gwp.tile([P, 8192], BF16, name="gw%d" % tau, tag="gw", align_bytes=64)
-            gwv = gw[:].bitcast(F32).rearrange("p (m c u) -> p m c u", m=8, c=256, u=2)
-            src = w_raw[tau][:].rearrange("p (u k o) -> p u k o", u=2, k=256, o=16)
-            l2s = []
-            for ob in range(4):
-                l2 = l2p.tile([P, 2048], BF16, name="l2_%d_%d" % (tau, ob), tag="l2")
-                l2s.append(l2)
-            if split_u:
-                for u in range(2):
-                    for ob in range(4):
-                        dst = l2s[ob][:].rearrange("p (u i k) -> p u k i", u=2, i=4, k=256)
-                        nc.vector.tensor_copy(
-                            out=dst[:, u], in_=src[:, u, :, 4 * ob : 4 * ob + 4]
-                        )
-            for ob in range(4):
-                if not split_u:
-                    dst = l2s[ob][:].rearrange("p (u i k) -> p u k i", u=2, i=4, k=256)
-                    nc.vector.tensor_copy(out=dst, in_=src[:, :, :, 4 * ob : 4 * ob + 4])
-                l2w = l2s[ob][:].bitcast(F32)
-                for jj in range(2):
-                    j = 2 * ob + jj
-                    bank = tp.tile([P, 512], F32, name="bw%d_%d" % (tau, j), tag="tp")
-                    for u in range(2):
-                        for oo in range(2):
-                            i = 2 * jj + oo
-                            nc.tensor.transpose(
-                                out=bank[:, (2 * u + oo) * P : (2 * u + oo + 1) * P],
-                                in_=l2w[:, (4 * u + i) * P : (4 * u + i + 1) * P],
-                                identity=ident[:],
-                            )
-                    nc.scalar.copy(
-                        out=gwv[:, :, 32 * j : 32 * j + 32, :],
-                        in_=bank[:].rearrange("p (u c m) -> p m c u", u=2, c=32, m=8),
+                for m in range(2):
+                    nc.sync.dma_start(
+                        out=x_raw[b][m][:, g0 * 512 : g1 * 512],
+                        in_=xf[b * P : (b + 1) * P, m * HALF_K + g0 * 512 : m * HALF_K + g1 * 512],
                     )
-            for half in range(2):
-                s0 = (8 * tau + 4 * half) * 256
-                nc.vector.quantize_mx(
-                    out=wc[:, s0 : s0 + 1024].bitcast(FP8X4),
-                    scales=ws[:, s0 : s0 + 1024],
-                    in_=gw[:, half * 4096 : (half + 1) * 4096],
-                )
 
-        def w_left():
-            gw = gwp.tile([P, 2048], BF16, name="gwl", tag="gwl", bufs=1, align_bytes=64)
-            gwv = gw[:].bitcast(F32).rearrange("p (m c u) -> p m c u", m=2, c=256, u=2)
-            src = w_rawl[:].rearrange("p (k o) -> p k o", k=256, o=16)
-            for ob in range(4):
-                l2 = l2p.tile([P, 1024], BF16, name="l2_l_%d" % ob, tag="l2")
-                nc.vector.tensor_copy(
-                    out=l2[:].rearrange("p (i k) -> p k i", i=4, k=256),
-                    in_=src[:, :, 4 * ob : 4 * ob + 4],
+        load_w(0)
+        load_w(1)
+        load_x(0, 2)
+        load_w(2)
+        load_x(2, 4)
+        load_w(3)
+        load_x(4, 6)
+        load_w(4)
+        load_x(6, 9)
+
+        xw = [[x_raw[b][m][:].bitcast(F32) for m in range(2)] for b in range(2)]
+        gws = {}
+        gxs = {}
+
+        def n_slots(s):
+            return 4 if s < LAST else 2
+
+        def w_piece(s, ob):
+            ns = n_slots(s)
+            if ob == 0:
+                gws[s] = gwp.tile([P, ns * 1024], BF16, name="gw%d" % s, tag="gw", align_bytes=64)
+            gwv = gws[s][:].bitcast(F32).rearrange("p (s c u) -> p s c u", s=ns, c=256, u=2)
+            l2 = l2p.tile([P, 1024], BF16, name="l2_%d_%d" % (s, ob), tag="l2")
+            nc.vector.tensor_copy(
+                out=l2[:].rearrange("p (i k) -> p k i", i=4, k=256),
+                in_=w_raw[s][:].rearrange("p (k o) -> p k o", k=256, o=16)[:, :, 4 * ob : 4 * ob + 4],
+            )
+            l2w = l2[:].bitcast(F32)
+            bank = tp.tile([P, 512], F32, name="bw%d_%d" % (s, ob), tag="tp")
+            for i in range(4):
+                nc.tensor.transpose(
+                    out=bank[:, i * P : (i + 1) * P],
+                    in_=l2w[:, i * P : (i + 1) * P],
+                    identity=ident[:],
                 )
-                l2w = l2[:].bitcast(F32)
-                bank = tp.tile([P, 512], F32, name="bwl%d" % ob, tag="tp")
-                for i in range(4):
+            if s < LAST:
+                src = bank[:].rearrange("p (c s u) -> p s c u", c=64, s=4, u=2)
+            else:
+                src = bank[:].rearrange("p (c m q) -> p m c q", c=64, m=2, q=4)[:, :, :, 0:2]
+            nc.scalar.copy(out=gwv[:, :, 64 * ob : 64 * ob + 64, :], in_=src)
+
+        def w_quant(s):
+            ns = n_slots(s)
+            nc.vector.quantize_mx(
+                out=wc[:, s * 1024 : s * 1024 + ns * 256].bitcast(FP8X4),
+                scales=ws[:, s * 1024 : s * 1024 + ns * 256],
+                in_=gws[s][:],
+            )
+
+        def x_off(s, b):
+            return s * 1024 + b * n_slots(s) * P
+
+        def x_pieces(s):
+            if s < LAST:
+                return [(b, m) for b in range(2) for m in range(2)]
+            return [(b, 0) for b in range(2)]
+
+        def x_piece(s, b, m):
+            ns = n_slots(s)
+            if m == 0:
+                gxs[(s, b)] = gxp.tile(
+                    [P, ns * 512], BF16, name="gx%d_%d" % (s, b), tag="gx", align_bytes=64
+                )
+            gxv = gxs[(s, b)][:].bitcast(F32).rearrange("p (s b u) -> p s b u", s=ns, b=P, u=2)
+            bank = tp.tile([P, 512], F32, name="bx%d_%d_%d" % (s, b, m), tag="tp")
+            for l in range(2):
+                half, g = (m, 2 * s + l) if s < LAST else (l, 8)
+                for u in range(2):
+                    c0 = 256 * g + P * u
                     nc.tensor.transpose(
-                        out=bank[:, i * P : (i + 1) * P],
-                        in_=l2w[:, i * P : (i + 1) * P],
+                        out=bank[:, (2 * l + u) * P : (2 * l + u + 1) * P],
+                        in_=xw[b][half][:, c0 : c0 + P],
                         identity=ident[:],
                     )
-                nc.scalar.copy(
-                    out=gwv[:, :, 64 * ob : 64 * ob + 64, :],
-                    in_=bank[:].rearrange("p (c m q) -> p m c q", c=64, m=2, q=4)[:, :, :, 0:2],
-                )
-            nc.vector.quantize_mx(
-                out=wc[:, 16 * 256 : 18 * 256].bitcast(FP8X4),
-                scales=ws[:, 16 * 256 : 18 * 256],
-                in_=gw[:],
+            nc.scalar.copy(
+                out=gxv[:, 2 * m : 2 * m + 2, :, :],
+                in_=bank[:].rearrange("p (l u b) -> p l b u", l=2, u=2, b=P),
             )
 
-        def x_off(slot, b):
-            if slot >= 16:
-                return 4096 + b * 256 + (slot - 16) * P
-            gi, sl = divmod(slot, 4)
-            return gi * 1024 + b * 512 + sl * P
-
-        def x_job(slots, b):
-            ns = len(slots)
-            gx = gxp.tile(
-                [P, ns * 512], BF16, name="gx%d_%d" % (slots[0], b), tag="gx", align_bytes=64
-            )
-            gxv = gx[:].bitcast(F32).rearrange("p (s b u) -> p s b u", s=ns, b=P, u=2)
-            for lp in range(ns // 2):
-                bank = tp.tile([P, 512], F32, name="bx%d_%d_%d" % (slots[0], b, lp), tag="tp")
-                for l in range(2):
-                    g = pass_of_slot(slots[2 * lp + l])
-                    for u in range(2):
-                        c0 = 256 * g + P * u
-                        nc.tensor.transpose(
-                            out=bank[:, (2 * l + u) * P : (2 * l + u + 1) * P],
-                            in_=xw[b][:, c0 : c0 + P],
-                            identity=ident[:],
-                        )
-                nc.scalar.copy(
-                    out=gxv[:, 2 * lp : 2 * lp + 2, :, :],
-                    in_=bank[:].rearrange("p (l u b) -> p l b u", l=2, u=2, b=P),
-                )
-            o0 = x_off(slots[0], b)
+        def x_quant(s, b):
+            ns = n_slots(s)
+            o0 = x_off(s, b)
             nc.vector.quantize_mx(
                 out=xc[:, o0 : o0 + ns * P].bitcast(FP8X4),
                 scales=xs[:, o0 : o0 + ns * P],
-                in_=gx[:],
+                in_=gxs[(s, b)][:],
             )
 
-        def mm(slot):
-            for b in range(2):
-                o0 = x_off(slot, b)
-                nc.tensor.matmul_mx(
-                    out=acc[b][:],
-                    lhsT=xc[:, o0 : o0 + P].bitcast(FP8X4),
-                    lhsT_scale=xs[:, o0 : o0 + P],
-                    rhs=wc[:, slot * 256 : (slot + 1) * 256].bitcast(FP8X4),
-                    rhs_scale=ws[:, slot * 256 : (slot + 1) * 256],
-                    start=(slot == 0),
-                    stop=(slot == 17),
-                )
+        def mm(s, halves):
+            for sl in range(n_slots(s)):
+                for b in halves:
+                    o0 = x_off(s, b) + sl * P
+                    w0 = s * 1024 + sl * 256
+                    nc.tensor.matmul_mx(
+                        out=acc[b][:],
+                        lhsT=xc[:, o0 : o0 + P].bitcast(FP8X4),
+                        lhsT_scale=xs[:, o0 : o0 + P],
+                        rhs=wc[:, w0 : w0 + 256].bitcast(FP8X4),
+                        rhs_scale=ws[:, w0 : w0 + 256],
+                        start=(s == 0 and sl == 0),
+                        stop=(s == 3 and sl == 3),
+                    )
 
-        w_main(0, True)
-        w_left()
-        for m in range(2):
-            for b in range(2):
-                x_job([4 * m + s for s in range(4)], b)
-        for slot in range(8):
-            mm(slot)
-        w_main(1, False)
-        for m in range(2):
-            for b in range(2):
-                x_job([8 + 4 * m + s for s in range(4)], b)
-        for b in range(2):
-            x_job([16, 17], b)
-        for slot in range(8, 18):
-            mm(slot)
+        def keep_busy():
+            for d in range(1):
+                nc.tensor.matmul(out=idle[:], lhsT=ident[:], rhs=ident[:], start=True, stop=True)
+
+        for i in range(STAGES):
+            if i >= 3:
+                mm(i - 3, (0, 1))
+            xp = x_pieces(i - 1) if i >= 1 else []
+            for ob in range(4):
+                w_piece(i, ob)
+                if ob < len(xp):
+                    x_piece(i - 1, xp[ob][0], xp[ob][1])
+                keep_busy()
+            if i == LAST:
+                x_piece(LAST, 0, 0)
+                x_piece(LAST, 1, 0)
+            if i >= 1:
+                w_quant(i - 1)
+            if i >= 2:
+                x_quant(i - 2, 0)
+                x_quant(i - 2, 1)
+        mm(2, (0, 1))
+        w_quant(LAST)
+        x_quant(LAST, 0)
+        x_quant(LAST, 1)
+        mm(LAST, (0, 1))
+        x_quant(3, 0)
+        mm(3, (0,))
+        x_quant(3, 1)
+        mm(3, (1,))
 
         outv = out.rearrange("n b x y o -> b n (x y o)")
+        s2 = [ep.tile([P, 256], F32, name="s2_%d" % b, tag="s2") for b in range(2)]
+        sq = [ep.tile([P, 16], F32, name="sq%d" % b, tag="sq") for b in range(2)]
+        rt = [ep.tile([P, 16], F32, name="rt%d" % b, tag="rt") for b in range(2)]
+        den = [ep.tile([P, 16], F32, name="den%d" % b, tag="den") for b in range(2)]
+        fac = [ep.tile([P, 16], F32, name="fac%d" % b, tag="fac") for b in range(2)]
+        res = [ep.tile([P, 256], F32, name="res%d" % b, tag="res") for b in range(2)]
         for b in range(2):
-            s = ep.tile([P, 256], F32, name="s%d" % b, tag="s")
-            sv = s[:].rearrange("p (n o) -> p n o", n=16, o=16)
-            nc.scalar.mul(
-                out=sv,
-                in_=acc[b][:].rearrange("p (o n) -> p n o", o=16, n=16),
-                mul=1.0 / ROUTES,
-            )
-            s2 = ep.tile([P, 256], F32, name="s2_%d" % b, tag="s2")
-            nc.vector.tensor_tensor(out=s2[:], in0=s[:], in1=s[:], op=ALU.mult)
-            sq = ep.tile([P, 16], F32, name="sq%d" % b, tag="sq")
+            nc.scalar.activation(out=s2[b][:], in_=acc[b][:], func=ACT.Square, scale=1.0 / ROUTES)
             nc.vector.tensor_reduce(
-                out=sq[:],
-                in_=s2[:].rearrange("p (n o) -> p n o", n=16, o=16),
+                out=sq[b][:],
+                in_=s2[b][:].rearrange("p (o n) -> p n o", o=16, n=16),
                 axis=mybir.AxisListType.X,
                 op=ALU.add,
             )
-            rt = ep.tile([P, 16], F32, name="rt%d" % b, tag="rt")
-            nc.scalar.activation(out=rt[:], in_=sq[:], func=ACT.Sqrt)
-            den = ep.tile([P, 16], F32, name="den%d" % b, tag="den")
-            nc.vector.tensor_scalar_add(den[:], sq[:], 1.0)
-            nc.vector.reciprocal(den[:], den[:])
-            fac = ep.tile([P, 16], F32, name="fac%d" % b, tag="fac")
-            nc.vector.tensor_tensor(out=fac[:], in0=rt[:], in1=den[:], op=ALU.mult)
-            res = ep.tile([P, 256], F32, name="res%d" % b, tag="res")
+            nc.scalar.activation(out=rt[b][:], in_=sq[b][:], func=ACT.Sqrt)
+            nc.vector.tensor_scalar_add(den[b][:], sq[b][:], 1.0)
+            nc.vector.reciprocal(den[b][:], den[b][:])
+        for b in range(2):
+            nc.vector.scalar_tensor_tensor(
+                out=fac[b][:],
+                in0=rt[b][:],
+                scalar=1.0 / ROUTES,
+                in1=den[b][:],
+                op0=ALU.mult,
+                op1=ALU.mult,
+            )
             nc.vector.tensor_tensor(
-                out=res[:].rearrange("p (n o) -> p n o", n=16, o=16),
-                in0=sv,
-                in1=fac[:].unsqueeze(2).to_broadcast([P, 16, 16]),
+                out=res[b][:].rearrange("p (n o) -> p n o", n=16, o=16),
+                in0=acc[b][:].rearrange("p (o n) -> p n o", o=16, n=16),
+                in1=fac[b][:].unsqueeze(2).to_broadcast([P, 16, 16]),
                 op=ALU.mult,
             )
             nc.sync.dma_start(
                 out=outv[b * P : (b + 1) * P],
-                in_=res[:].rearrange("p (n o) -> p n o", n=16, o=16),
+                in_=res[b][:].rearrange("p (n o) -> p n o", n=16, o=16),
             )

@@ -51,7 +51,7 @@ def tile_capsulelayer_kernel(tc, x, W, out):
         xc = keep.tile([P, 18 * 256], U32, align_bytes=64)
         xs = keep.tile([P, 18 * 256], U8, align_bytes=64)
         acc = [accp.tile([P, 256], F32, name="acc%d" % b) for b in range(2)]
-        idle = accp.tile([P, P], F32, name="idle")
+
 
         nc.vector.memset(w_raw[LAST][:], 0.0)
 
@@ -174,10 +174,6 @@ def tile_capsulelayer_kernel(tc, x, W, out):
                         stop=(s == 3 and sl == 3),
                     )
 
-        def keep_busy():
-            for d in range(1):
-                nc.tensor.matmul(out=idle[:], lhsT=ident[:], rhs=ident[:], start=True, stop=True)
-
         for i in range(STAGES):
             if i >= 3:
                 mm(i - 3, (0, 1))
@@ -186,7 +182,6 @@ def tile_capsulelayer_kernel(tc, x, W, out):
                 w_piece(i, ob)
                 if ob < len(xp):
                     x_piece(i - 1, xp[ob][0], xp[ob][1])
-                keep_busy()
             if i == LAST:
                 x_piece(LAST, 0, 0)
                 x_piece(LAST, 1, 0)

@@ -171,10 +171,10 @@ def tile_capsulelayer_kernel(tc, x, W, out):
                         rhs=wc[:, w0 : w0 + 256].bitcast(FP8X4),
                         rhs_scale=ws[:, w0 : w0 + 256],
                         start=(s == 0 and sl == 0),
-                        stop=(s == 3 and sl == 3),
+                        stop=(s == LAST and sl == 1),
                     )
 
-        for i in range(STAGES):
+        for i in range(LAST):
             if i >= 3:
                 mm(i - 3, (0, 1))
             xp = x_pieces(i - 1) if i >= 1 else []
@@ -182,23 +182,32 @@ def tile_capsulelayer_kernel(tc, x, W, out):
                 w_piece(i, ob)
                 if ob < len(xp):
                     x_piece(i - 1, xp[ob][0], xp[ob][1])
-            if i == LAST:
-                x_piece(LAST, 0, 0)
-                x_piece(LAST, 1, 0)
             if i >= 1:
                 w_quant(i - 1)
             if i >= 2:
                 x_quant(i - 2, 0)
                 x_quant(i - 2, 1)
+        mm(1, (0, 1))
+        w_piece(LAST, 0)
+        x_piece(3, 0, 0)
+        w_piece(LAST, 1)
+        x_piece(3, 0, 1)
+        w_piece(LAST, 2)
+        x_piece(LAST, 0, 0)
+        w_piece(LAST, 3)
+        x_piece(3, 1, 0)
+        x_piece(3, 1, 1)
+        x_piece(LAST, 1, 0)
+        w_quant(3)
+        x_quant(2, 0)
+        x_quant(2, 1)
         mm(2, (0, 1))
         w_quant(LAST)
-        x_quant(LAST, 0)
-        x_quant(LAST, 1)
-        mm(LAST, (0, 1))
-        x_quant(3, 0)
-        mm(3, (0,))
-        x_quant(3, 1)
-        mm(3, (1,))
+        for b in range(2):
+            x_quant(3, b)
+            x_quant(LAST, b)
+            mm(3, (b,))
+            mm(LAST, (b,))
 
         outv = out.rearrange("n b x y o -> b n (x y o)")
         s2 = [ep.tile([P, 256], F32, name="s2_%d" % b, tag="s2") for b in range(2)]
@@ -218,7 +227,6 @@ def tile_capsulelayer_kernel(tc, x, W, out):
             nc.scalar.activation(out=rt[b][:], in_=sq[b][:], func=ACT.Sqrt)
             nc.vector.tensor_scalar_add(den[b][:], sq[b][:], 1.0)
             nc.vector.reciprocal(den[b][:], den[b][:])
-        for b in range(2):
             nc.vector.scalar_tensor_tensor(
                 out=fac[b][:],
                 in0=rt[b][:],

@@ -216,17 +216,25 @@ def tile_capsulelayer_kernel(tc, x, W, out):
         den = [ep.tile([P, 16], F32, name="den%d" % b, tag="den") for b in range(2)]
         fac = [ep.tile([P, 16], F32, name="fac%d" % b, tag="fac") for b in range(2)]
         res = [ep.tile([P, 256], F32, name="res%d" % b, tag="res") for b in range(2)]
-        for b in range(2):
+        def square(b):
             nc.scalar.activation(out=s2[b][:], in_=acc[b][:], func=ACT.Square, scale=1.0 / ROUTES)
+
+        def reduce(b):
             nc.vector.tensor_reduce(
                 out=sq[b][:],
                 in_=s2[b][:].rearrange("p (o n) -> p n o", o=16, n=16),
                 axis=mybir.AxisListType.X,
                 op=ALU.add,
             )
+
+        def root(b):
             nc.scalar.activation(out=rt[b][:], in_=sq[b][:], func=ACT.Sqrt)
+
+        def denom(b):
             nc.vector.tensor_scalar_add(den[b][:], sq[b][:], 1.0)
             nc.vector.reciprocal(den[b][:], den[b][:])
+
+        def factor(b):
             nc.vector.scalar_tensor_tensor(
                 out=fac[b][:],
                 in0=rt[b][:],
@@ -235,6 +243,8 @@ def tile_capsulelayer_kernel(tc, x, W, out):
                 op0=ALU.mult,
                 op1=ALU.mult,
             )
+
+        def scale_store(b):
             nc.vector.tensor_tensor(
                 out=res[b][:].rearrange("p (n o) -> p n o", n=16, o=16),
                 in0=acc[b][:].rearrange("p (o n) -> p n o", o=16, n=16),
@@ -245,3 +255,16 @@ def tile_capsulelayer_kernel(tc, x, W, out):
                 out=outv[b * P : (b + 1) * P],
                 in_=res[b][:].rearrange("p (n o) -> p n o", n=16, o=16),
             )
+
+        square(0)
+        reduce(0)
+        denom(0)
+        square(1)
+        root(0)
+        reduce(1)
+        factor(0)
+        denom(1)
+        root(1)
+        scale_store(0)
+        factor(1)
+        scale_store(1)

@@ -53,15 +53,20 @@ def tile_capsulelayer_kernel(tc, x, W, out):
         acc = [accp.tile([P, 256], F32, name="acc%d" % b) for b in range(2)]
 
 
-        nc.vector.memset(w_raw[LAST][:], 0.0)
-
         wr = W.rearrange("n (m r) i o -> (n m) (r i o)", m=2)
         xf = x.rearrange("b r i -> b (r i)")
 
         def load_w(s):
-            for q in range(4 if s < LAST else 2):
-                c0 = (4 * s + q) * 4096
-                nc.sync.dma_start(out=w_raw[s][q:P:4, :], in_=wr[:, c0 : c0 + 4096])
+            for q in range(4):
+                if s < LAST:
+                    c0 = (4 * s + q) * 4096
+                    nc.sync.dma_start(out=w_raw[s][q:P:4, :], in_=wr[:, c0 : c0 + 4096])
+                else:
+                    c0 = (4 * s + q % 2) * 4096
+                    shift = 8 * (q // 2)
+                    nc.sync.dma_start(
+                        out=w_raw[s][q:P:4, 0 : 4096 - shift], in_=wr[:, c0 + shift : c0 + 4096]
+                    )
 
         def load_x(g0, g1):
             for b in range(2):
@@ -108,9 +113,11 @@ def tile_capsulelayer_kernel(tc, x, W, out):
                 )
             if s < LAST:
                 src = bank[:].rearrange("p (c s u) -> p s c u", c=64, s=4, u=2)
+                dst = gwv[:, :, 64 * ob : 64 * ob + 64, :]
             else:
-                src = bank[:].rearrange("p (c m q) -> p m c q", c=64, m=2, q=4)[:, :, :, 0:2]
-            nc.scalar.copy(out=gwv[:, :, 64 * ob : 64 * ob + 64, :], in_=src)
+                src = bank[:].rearrange("p (c m h u) -> p m h c u", c=64, m=2, h=2, u=2)
+                dst = gwv.rearrange("p s (h g c) u -> p s h g c u", h=2, g=2, c=64)[:, :, :, ob, :, :]
+            nc.scalar.copy(out=dst, in_=src)
 
         def w_quant(s):
             ns = n_slots(s)
@@ -192,9 +199,7 @@ def tile_capsulelayer_kernel(tc, x, W, out):
         x_piece(3, 0, 0)
         w_piece(LAST, 1)
         x_piece(3, 0, 1)
-        w_piece(LAST, 2)
         x_piece(LAST, 0, 0)
-        w_piece(LAST, 3)
         x_piece(3, 1, 0)
         x_piece(3, 1, 1)
         x_piece(LAST, 1, 0)

@@ -68,8 +68,8 @@ def tile_capsulelayer_kernel(tc, x, W, out):
                         out=w_raw[s][q:P:4, 0 : 4096 - shift], in_=wr[:, c0 + shift : c0 + 4096]
                     )
 
-        def load_x(g0, g1):
-            for b in range(2):
+        def load_x(g0, g1, halves=(0, 1)):
+            for b in halves:
                 for m in range(2):
                     nc.sync.dma_start(
                         out=x_raw[b][m][:, g0 * 512 : g1 * 512],
@@ -84,7 +84,9 @@ def tile_capsulelayer_kernel(tc, x, W, out):
         load_w(3)
         load_x(4, 6)
         load_w(4)
-        load_x(6, 9)
+        load_x(6, 9, (0,))
+        load_x(6, 8, (1,))
+        load_x(8, 9, (1,))
 
         xw = [[x_raw[b][m][:].bitcast(F32) for m in range(2)] for b in range(2)]
         gws = {}

@@ -196,26 +196,6 @@ def tile_capsulelayer_kernel(tc, x, W, out):
             if i >= 2:
                 x_quant(i - 2, 0)
                 x_quant(i - 2, 1)
-        mm(1, (0, 1))
-        w_piece(LAST, 0)
-        x_piece(3, 0, 0)
-        w_piece(LAST, 1)
-        x_piece(3, 0, 1)
-        x_piece(LAST, 0, 0)
-        x_piece(3, 1, 0)
-        x_piece(3, 1, 1)
-        x_piece(LAST, 1, 0)
-        w_quant(3)
-        x_quant(2, 0)
-        x_quant(2, 1)
-        mm(2, (0, 1))
-        w_quant(LAST)
-        for b in range(2):
-            x_quant(3, b)
-            x_quant(LAST, b)
-            mm(3, (b,))
-            mm(LAST, (b,))
-
         outv = out.rearrange("n b x y o -> b n (x y o)")
         s2 = [ep.tile([P, 256], F32, name="s2_%d" % b, tag="s2") for b in range(2)]
         sq = [ep.tile([P, 16], F32, name="sq%d" % b, tag="sq") for b in range(2)]
@@ -263,15 +243,34 @@ def tile_capsulelayer_kernel(tc, x, W, out):
                 in_=res[b][:].rearrange("p (n o) -> p n o", n=16, o=16),
             )
 
+        mm(1, (0, 1))
+        w_piece(LAST, 0)
+        x_piece(3, 0, 0)
+        w_piece(LAST, 1)
+        x_piece(3, 0, 1)
+        x_piece(LAST, 0, 0)
+        x_piece(3, 1, 0)
+        x_piece(3, 1, 1)
+        x_piece(LAST, 1, 0)
+        w_quant(3)
+        x_quant(2, 0)
+        w_quant(LAST)
+        x_quant(3, 0)
+        x_quant(LAST, 0)
+        for s in (2, 3, LAST):
+            mm(s, (0,))
+        for s in (2, 3, LAST):
+            x_quant(s, 1)
+            mm(s, (1,))
         square(0)
         reduce(0)
         denom(0)
-        square(1)
         root(0)
-        reduce(1)
+        square(1)
         factor(0)
+        reduce(1)
+        scale_store(0)
         denom(1)
         root(1)
-        scale_store(0)
         factor(1)
         scale_store(1)

from contextlib import ExitStack

import concourse.masks as masks
import concourse.mybir as mybir

FLOPS = 2 * 256 * 9216 * 256

F32 = mybir.dt.float32
BF16 = mybir.dt.bfloat16
U32 = mybir.dt.uint32
U8 = mybir.dt.uint8
FP8X4 = mybir.dt.float8_e4m3fn_x4
ACT = mybir.ActivationFunctionType
ALU = mybir.AluOpType

P = 128
HALF_K = 4608
ROUTES = 1152
STAGES = 5
LAST = 4


def tile_capsulelayer_kernel(tc, x, W, out):
    nc = tc.nc
    with ExitStack() as ctx:
        const = ctx.enter_context(tc.tile_pool(name="const", bufs=1))
        raw = ctx.enter_context(tc.tile_pool(name="raw", bufs=1))
        keep = ctx.enter_context(tc.tile_pool(name="keep", bufs=1))
        l2p = ctx.enter_context(tc.tile_pool(name="l2p", bufs=6))
        gwp = ctx.enter_context(tc.tile_pool(name="gwp", bufs=3))
        gxp = ctx.enter_context(tc.tile_pool(name="gxp", bufs=6))
        ep = ctx.enter_context(tc.tile_pool(name="ep", bufs=2))
        tp = ctx.enter_context(tc.psum_pool(name="tp", bufs=5))
        accp = ctx.enter_context(tc.psum_pool(name="accp", bufs=1))
        ctx.enter_context(tc.manual_schedule())

        ident = const.tile([P, P], F32)
        masks.make_identity(nc, ident[:])
        one = const.tile([P, 1], F32)
        nc.vector.memset(one[:], 1.0)
        warm = const.tile([P, 1], F32)
        nc.scalar.activation(out=warm[:], in_=one[:], func=ACT.Sqrt)

        w_raw = [raw.tile([P, 4096], BF16, name="w_raw%d" % s) for s in range(STAGES)]
        x_raw = [
            [raw.tile([P, HALF_K], BF16, name="x_raw%d_%d" % (b, m)) for m in range(2)]
            for b in range(2)
        ]
        wc = keep.tile([P, 18 * 256], U32, align_bytes=64)
        ws = keep.tile([P, 18 * 256], U8, align_bytes=64)
        xc = keep.tile([P, 18 * 256], U32, align_bytes=64)
        xs = keep.tile([P, 18 * 256], U8, align_bytes=64)
        acc = [accp.tile([P, 256], F32, name="acc%d" % b) for b in range(2)]


        wr = W.rearrange("n (m r) i o -> (n m) (r i o)", m=2)
        xf = x.rearrange("b r i -> b (r i)")

        def load_w(s):
            for q in range(4):
                if s < LAST:
                    c0 = (4 * s + q) * 4096
                    nc.sync.dma_start(out=w_raw[s][q:P:4, :], in_=wr[:, c0 : c0 + 4096])
                else:
                    c0 = (4 * s + q % 2) * 4096
                    shift = 8 * (q // 2)
                    nc.sync.dma_start(
                        out=w_raw[s][q:P:4, 0 : 4096 - shift], in_=wr[:, c0 + shift : c0 + 4096]
                    )

        def load_x(g0, g1, halves=(0, 1)):
            for b in halves:
                for m in range(2):
                    nc.sync.dma_start(
                        out=x_raw[b][m][:, g0 * 512 : g1 * 512],
                        in_=xf[b * P : (b + 1) * P, m * HALF_K + g0 * 512 : m * HALF_K + g1 * 512],
                    )

        load_w(0)
        load_w(1)
        load_x(0, 2)
        load_w(2)
        load_x(2, 4)
        load_w(3)
        load_x(4, 6)
        load_w(4)
        load_x(6, 9, (0,))
        load_x(6, 8, (1,))
        load_x(8, 9, (1,))

        xw = [[x_raw[b][m][:].bitcast(F32) for m in range(2)] for b in range(2)]
        gws = {}
        gxs = {}

        def n_slots(s):
            return 4 if s < LAST else 2

        def w_piece(s, ob):
            ns = n_slots(s)
            if ob == 0:
                gws[s] = gwp.tile([P, ns * 1024], BF16, name="gw%d" % s, tag="gw", align_bytes=64)
            gwv = gws[s][:].bitcast(F32).rearrange("p (s c u) -> p s c u", s=ns, c=256, u=2)
            l2 = l2p.tile([P, 1024], BF16, name="l2_%d_%d" % (s, ob), tag="l2")
            nc.vector.tensor_copy(
                out=l2[:].rearrange("p (i k) -> p k i", i=4, k=256),
                in_=w_raw[s][:].rearrange("p (k o) -> p k o", k=256, o=16)[:, :, 4 * ob : 4 * ob + 4],
            )
            l2w = l2[:].bitcast(F32)
            bank = tp.tile([P, 512], F32, name="bw%d_%d" % (s, ob), tag="tp")
            for i in range(4):
                nc.tensor.transpose(
                    out=bank[:, i * P : (i + 1) * P],
                    in_=l2w[:, i * P : (i + 1) * P],
                    identity=ident[:],
                )
            if s < LAST:
                src = bank[:].rearrange("p (c s u) -> p s c u", c=64, s=4, u=2)
                dst = gwv[:, :, 64 * ob : 64 * ob + 64, :]
            else:
                src = bank[:].rearrange("p (c m h u) -> p m h c u", c=64, m=2, h=2, u=2)
                dst = gwv.rearrange("p s (h g c) u -> p s h g c u", h=2, g=2, c=64)[:, :, :, ob, :, :]
            nc.scalar.copy(out=dst, in_=src)

        def w_quant(s):
            ns = n_slots(s)
            nc.vector.quantize_mx(
                out=wc[:, s * 1024 : s * 1024 + ns * 256].bitcast(FP8X4),
                scales=ws[:, s * 1024 : s * 1024 + ns * 256],
                in_=gws[s][:],
            )

        def x_off(s, b):
            return s * 1024 + b * n_slots(s) * P

        def x_pieces(s):
            if s < LAST:
                return [(b, m) for b in range(2) for m in range(2)]
            return [(b, 0) for b in range(2)]

        def x_piece(s, b, m):
            ns = n_slots(s)
            if m == 0:
                gxs[(s, b)] = gxp.tile(
                    [P, ns * 512], BF16, name="gx%d_%d" % (s, b), tag="gx", align_bytes=64
                )
            gxv = gxs[(s, b)][:].bitcast(F32).rearrange("p (s b u) -> p s b u", s=ns, b=P, u=2)
            bank = tp.tile([P, 512], F32, name="bx%d_%d_%d" % (s, b, m), tag="tp")
            for l in range(2):
                half, g = (m, 2 * s + l) if s < LAST else (l, 8)
                for u in range(2):
                    c0 = 256 * g + P * u
                    nc.tensor.transpose(
                        out=bank[:, (2 * l + u) * P : (2 * l + u + 1) * P],
                        in_=xw[b][half][:, c0 : c0 + P],
                        identity=ident[:],
                    )
            nc.scalar.copy(
                out=gxv[:, 2 * m : 2 * m + 2, :, :],
                in_=bank[:].rearrange("p (l u b) -> p l b u", l=2, u=2, b=P),
            )

        def x_quant(s, b):
            ns = n_slots(s)
            o0 = x_off(s, b)
            nc.vector.quantize_mx(
                out=xc[:, o0 : o0 + ns * P].bitcast(FP8X4),
                scales=xs[:, o0 : o0 + ns * P],
                in_=gxs[(s, b)][:],
            )

        def mm(s, halves):
            for sl in range(n_slots(s)):
                for b in halves:
                    o0 = x_off(s, b) + sl * P
                    w0 = s * 1024 + sl * 256
                    nc.tensor.matmul_mx(
                        out=acc[b][:],
                        lhsT=xc[:, o0 : o0 + P].bitcast(FP8X4),
                        lhsT_scale=xs[:, o0 : o0 + P],
                        rhs=wc[:, w0 : w0 + 256].bitcast(FP8X4),
                        rhs_scale=ws[:, w0 : w0 + 256],
                        start=(s == 0 and sl == 0),
                        stop=(s == LAST and sl == 1),
                    )

        for i in range(LAST):
            if i >= 3:
                mm(i - 3, (0, 1))
            xp = x_pieces(i - 1) if i >= 1 else []
            for ob in range(4):
                w_piece(i, ob)
                if ob < len(xp):
                    x_piece(i - 1, xp[ob][0], xp[ob][1])
            if i >= 1:
                w_quant(i - 1)
            if i >= 2:
                x_quant(i - 2, 0)
                x_quant(i - 2, 1)
        outv = out.rearrange("n b x y o -> b n (x y o)")
        s2 = [ep.tile([P, 256], F32, name="s2_%d" % b, tag="s2") for b in range(2)]
        sq = [ep.tile([P, 16], F32, name="sq%d" % b, tag="sq") for b in range(2)]
        rt = [ep.tile([P, 16], F32, name="rt%d" % b, tag="rt") for b in range(2)]
        den = [ep.tile([P, 16], F32, name="den%d" % b, tag="den") for b in range(2)]
        fac = [ep.tile([P, 16], F32, name="fac%d" % b, tag="fac") for b in range(2)]
        res = [ep.tile([P, 256], F32, name="res%d" % b, tag="res") for b in range(2)]
        def square(b):
            nc.scalar.activation(out=s2[b][:], in_=acc[b][:], func=ACT.Square, scale=1.0 / ROUTES)

        def reduce(b):
            nc.vector.tensor_reduce(
                out=sq[b][:],
                in_=s2[b][:].rearrange("p (o n) -> p n o", o=16, n=16),
                axis=mybir.AxisListType.X,
                op=ALU.add,
            )

        def root(b):
            nc.scalar.activation(out=rt[b][:], in_=sq[b][:], func=ACT.Sqrt)

        def denom(b):
            nc.vector.tensor_scalar_add(den[b][:], sq[b][:], 1.0)
            nc.vector.reciprocal(den[b][:], den[b][:])

        def factor(b):
            nc.vector.scalar_tensor_tensor(
                out=fac[b][:],
                in0=rt[b][:],
                scalar=1.0 / ROUTES,
                in1=den[b][:],
                op0=ALU.mult,
                op1=ALU.mult,
            )

        def scale_store(b):
            nc.vector.tensor_tensor(
                out=res[b][:].rearrange("p (n o) -> p n o", n=16, o=16),
                in0=acc[b][:].rearrange("p (o n) -> p n o", o=16, n=16),
                in1=fac[b][:].unsqueeze(2).to_broadcast([P, 16, 16]),
                op=ALU.mult,
            )
            nc.sync.dma_start(
                out=outv[b * P : (b + 1) * P],
                in_=res[b][:].rearrange("p (n o) -> p n o", n=16, o=16),
            )

        mm(1, (0, 1))
        w_piece(LAST, 0)
        x_piece(3, 0, 0)
        w_piece(LAST, 1)
        x_piece(3, 0, 1)
        x_piece(LAST, 0, 0)
        x_piece(3, 1, 0)
        x_piece(3, 1, 1)
        x_piece(LAST, 1, 0)
        w_quant(3)
        x_quant(2, 0)
        w_quant(LAST)
        x_quant(3, 0)
        x_quant(LAST, 0)
        for s in (2, 3, LAST):
            mm(s, (0,))
        for s in (2, 3, LAST):
            x_quant(s, 1)
            mm(s, (1,))
        square(0)
        reduce(0)
        denom(0)
        root(0)
        square(1)
        factor(0)
        reduce(1)
        scale_store(0)
        denom(1)
        root(1)
        factor(1)
        scale_store(1)
